import numpy as np
import ml_dtypes

BF16 = ml_dtypes.bfloat16


def bf(x):
    return np.asarray(x, np.float32).astype(BF16)


def f32(x):
    return np.asarray(x, np.float32)


def f64(x):
    return np.asarray(x).astype(np.float64)


def striped(idx):
    return np.tile(idx.reshape(-1, 16).T, (8, 1))


D, S, N, M, H = 128, 1024, 512, 256, 4
SCALE = 1.0 / np.sqrt(D // H)


def setup_inputs():
    return {"sentences": bf(np.random.standard_normal((D, S))), "wk": bf(np.random.standard_normal((D, M)) / np.sqrt(D)), "mentions": bf(np.random.standard_normal((D, N))), "wv": bf(np.random.standard_normal((D, M)) / np.sqrt(D)), "offs": striped(np.random.permutation(np.tile(np.arange(S), 2))[:N])}


def reference(sentences, wk, mentions, wv, offs):
    idx = offs[:16].T.reshape(-1)
    keys = SCALE * (f64(wk).T @ f64(sentences)[:, idx])
    values = f64(wv).T @ f64(mentions)
    return np.concatenate([keys, values], axis=0)

@@ -1,0 +1,55 @@
+import math
+
+import concourse.mybir as mybir
+
+P = 128
+S = 1024
+N = 512
+M = 256
+BLOCKS = M // P
+SCALE = 1.0 / math.sqrt(32.0)
+
+FLOPS = 2 * P * N * (2 * M)
+BYTES = 2 * (P * N + P * M + P * N + P * M) + 2 * P * (N // 16) + 4 * (2 * M) * N
+
+BF16 = mybir.dt.bfloat16
+F32 = mybir.dt.float32
+U16 = mybir.dt.uint16
+COPY = mybir.ActivationFunctionType.Copy
+
+
+def tile_glremodule_kernel(tc, sentences, wk, mentions, wv, offs, out):
+    nc = tc.nc
+    with (
+        tc.tile_pool(name="held", bufs=1) as held,
+        tc.psum_pool(name="banks", bufs=1) as banks,
+    ):
+        offsets = held.tile([P, N // 16], U16, name="offsets")
+        nc.sync.dma_start(offsets[:], offs)
+
+        wv_sb = held.tile([P, M], BF16, name="wv_sb")
+        nc.scalar.dma_start(wv_sb[:], wv)
+        mentions_sb = held.tile([P, N], BF16, name="mentions_sb")
+        nc.scalar.dma_start(mentions_sb[:], mentions)
+        wk_sb = held.tile([P, M], BF16, name="wk_sb")
+        nc.sync.dma_start(wk_sb[:], wk)
+        window = held.tile([P, S], BF16, name="window")
+        nc.sync.dma_start(window[:], sentences)
+
+        for part, row0, scale in (("values", M, 1.0), ("keys", 0, SCALE)):
+            for b in range(BLOCKS):
+                cols = slice(b * P, (b + 1) * P)
+                bank = banks.tile([P, N], F32, name=f"{part}_bank{b}")
+                if part == "keys":
+                    nc.tensor.matmul(bank[:], wk_sb[:, cols], window[:].indirect(offsets[:]))
+                else:
+                    nc.tensor.matmul(bank[:], wv_sb[:, cols], mentions_sb[:])
+
+                staged = held.tile([P, N], F32, name=f"{part}_staged{b}")
+                rows = out[row0 + b * P : row0 + (b + 1) * P, :]
+                if b % 2 == 0:
+                    nc.vector.tensor_scalar_mul(staged[:], bank[:], scale)
+                    nc.sync.dma_start(rows, staged[:])
+                else:
+                    nc.scalar.activation(staged[:], bank[:], COPY, scale=scale)
+                    nc.scalar.dma_start(rows, staged[:])

@@ -24,15 +24,14 @@ def tile_glremodule_kernel(tc, sentences, wk, mentions, wv, offs, out):
         tc.tile_pool(name="held", bufs=1) as held,
         tc.psum_pool(name="banks", bufs=1) as banks,
     ):
-        offsets = held.tile([P, N // 16], U16, name="offsets")
-        nc.sync.dma_start(offsets[:], offs)
-
+        mentions_sb = held.tile([P, N], BF16, name="mentions_sb")
+        nc.sync.dma_start(mentions_sb[:], mentions)
         wv_sb = held.tile([P, M], BF16, name="wv_sb")
         nc.scalar.dma_start(wv_sb[:], wv)
-        mentions_sb = held.tile([P, N], BF16, name="mentions_sb")
-        nc.scalar.dma_start(mentions_sb[:], mentions)
+        offsets = held.tile([P, N // 16], U16, name="offsets")
+        nc.sync.dma_start(offsets[:], offs)
         wk_sb = held.tile([P, M], BF16, name="wk_sb")
-        nc.sync.dma_start(wk_sb[:], wk)
+        nc.scalar.dma_start(wk_sb[:], wk)
         window = held.tile([P, S], BF16, name="window")
         nc.sync.dma_start(window[:], sentences)
 

@@ -8,6 +8,7 @@ N = 512
 M = 256
 BLOCKS = M // P
 SCALE = 1.0 / math.sqrt(32.0)
+WARM_UP = 12
 
 FLOPS = 2 * P * N * (2 * M)
 BYTES = 2 * (P * N + P * M + P * N + P * M) + 2 * P * (N // 16) + 4 * (2 * M) * N
@@ -34,6 +35,12 @@ def tile_glremodule_kernel(tc, sentences, wk, mentions, wv, offs, out):
         nc.scalar.dma_start(wk_sb[:], wk)
         window = held.tile([P, S], BF16, name="window")
         nc.sync.dma_start(window[:], sentences)
+
+        zeros = held.tile([P, P], BF16, name="zeros")
+        nc.vector.memset(zeros[:], 0.0)
+        warm_bank = banks.tile([P, P], F32, name="warm_bank")
+        for w in range(WARM_UP):
+            nc.tensor.matmul(warm_bank[:], zeros[:], zeros[:])
 
         for part, row0, scale in (("values", M, 1.0), ("keys", 0, SCALE)):
             for b in range(BLOCKS):

@@ -7,8 +7,8 @@ S = 1024
 N = 512
 M = 256
 BLOCKS = M // P
+HALF = N // 2
 SCALE = 1.0 / math.sqrt(32.0)
-WARM_UP = 12
 
 FLOPS = 2 * P * N * (2 * M)
 BYTES = 2 * (P * N + P * M + P * N + P * M) + 2 * P * (N // 16) + 4 * (2 * M) * N
@@ -36,26 +36,21 @@ def tile_glremodule_kernel(tc, sentences, wk, mentions, wv, offs, out):
         window = held.tile([P, S], BF16, name="window")
         nc.sync.dma_start(window[:], sentences)
 
-        zeros = held.tile([P, P], BF16, name="zeros")
-        nc.vector.memset(zeros[:], 0.0)
-        warm_bank = banks.tile([P, P], F32, name="warm_bank")
-        for w in range(WARM_UP):
-            nc.tensor.matmul(warm_bank[:], zeros[:], zeros[:])
-
         for part, row0, scale in (("values", M, 1.0), ("keys", 0, SCALE)):
             for b in range(BLOCKS):
-                cols = slice(b * P, (b + 1) * P)
-                bank = banks.tile([P, N], F32, name=f"{part}_bank{b}")
-                if part == "keys":
-                    nc.tensor.matmul(bank[:], wk_sb[:, cols], window[:].indirect(offsets[:]))
-                else:
-                    nc.tensor.matmul(bank[:], wv_sb[:, cols], mentions_sb[:])
-
+                weight_cols = slice(b * P, (b + 1) * P)
                 staged = held.tile([P, N], F32, name=f"{part}_staged{b}")
-                rows = out[row0 + b * P : row0 + (b + 1) * P, :]
-                if b % 2 == 0:
-                    nc.vector.tensor_scalar_mul(staged[:], bank[:], scale)
-                    nc.sync.dma_start(rows, staged[:])
-                else:
-                    nc.scalar.activation(staged[:], bank[:], COPY, scale=scale)
-                    nc.scalar.dma_start(rows, staged[:])
+                for h in range(2):
+                    cols = slice(h * HALF, (h + 1) * HALF)
+                    bank = banks.tile([P, HALF], F32, name=f"{part}_bank{b}{h}")
+                    if part == "keys":
+                        piece = offsets[:, h * (HALF // 16) : (h + 1) * (HALF // 16)]
+                        nc.tensor.matmul(bank[:], wk_sb[:, weight_cols], window[:].indirect(piece))
+                    else:
+                        nc.tensor.matmul(bank[:], wv_sb[:, weight_cols], mentions_sb[:, cols])
+                    if h == 0:
+                        nc.vector.tensor_scalar_mul(staged[:, cols], bank[:], scale)
+                    else:
+                        nc.scalar.activation(staged[:, cols], bank[:], COPY, scale=scale)
+                queue = nc.sync if b % 2 == 0 else nc.scalar
+                queue.dma_start(out[row0 + b * P : row0 + (b + 1) * P, :], staged[:])

@@ -39,7 +39,6 @@ def tile_glremodule_kernel(tc, sentences, wk, mentions, wv, offs, out):
         for part, row0, scale in (("values", M, 1.0), ("keys", 0, SCALE)):
             for b in range(BLOCKS):
                 weight_cols = slice(b * P, (b + 1) * P)
-                staged = held.tile([P, N], F32, name=f"{part}_staged{b}")
                 for h in range(2):
                     cols = slice(h * HALF, (h + 1) * HALF)
                     bank = banks.tile([P, HALF], F32, name=f"{part}_bank{b}{h}")
@@ -48,9 +47,11 @@ def tile_glremodule_kernel(tc, sentences, wk, mentions, wv, offs, out):
                         nc.tensor.matmul(bank[:], wk_sb[:, weight_cols], window[:].indirect(piece))
                     else:
                         nc.tensor.matmul(bank[:], wv_sb[:, weight_cols], mentions_sb[:, cols])
+                    staged = held.tile([P, HALF], F32, name=f"{part}_staged{b}{h}")
+                    rows = out[row0 + b * P : row0 + (b + 1) * P, cols]
                     if h == 0:
-                        nc.vector.tensor_scalar_mul(staged[:, cols], bank[:], scale)
+                        nc.vector.tensor_scalar_mul(staged[:], bank[:], scale)
+                        nc.sync.dma_start(rows, staged[:])
                     else:
-                        nc.scalar.activation(staged[:, cols], bank[:], COPY, scale=scale)
-                queue = nc.sync if b % 2 == 0 else nc.scalar
-                queue.dma_start(out[row0 + b * P : row0 + (b + 1) * P, :], staged[:])
+                        nc.scalar.activation(staged[:], bank[:], COPY, scale=scale)
+                        nc.scalar.dma_start(rows, staged[:])

@@ -25,10 +25,11 @@ def tile_glremodule_kernel(tc, sentences, wk, mentions, wv, offs, out):
         tc.tile_pool(name="held", bufs=1) as held,
         tc.psum_pool(name="banks", bufs=1) as banks,
     ):
-        mentions_sb = held.tile([P, N], BF16, name="mentions_sb")
-        nc.sync.dma_start(mentions_sb[:], mentions)
+        mentions_half = [held.tile([P, HALF], BF16, name=f"mentions_half{h}") for h in range(2)]
+        nc.sync.dma_start(mentions_half[0][:], mentions[:, 0:HALF])
         wv_sb = held.tile([P, M], BF16, name="wv_sb")
         nc.scalar.dma_start(wv_sb[:], wv)
+        nc.scalar.dma_start(mentions_half[1][:], mentions[:, HALF:N])
         offsets = held.tile([P, N // 16], U16, name="offsets")
         nc.sync.dma_start(offsets[:], offs)
         wk_sb = held.tile([P, M], BF16, name="wk_sb")
@@ -46,7 +47,7 @@ def tile_glremodule_kernel(tc, sentences, wk, mentions, wv, offs, out):
                         piece = offsets[:, h * (HALF // 16) : (h + 1) * (HALF // 16)]
                         nc.tensor.matmul(bank[:], wk_sb[:, weight_cols], window[:].indirect(piece))
                     else:
-                        nc.tensor.matmul(bank[:], wv_sb[:, weight_cols], mentions_sb[:, cols])
+                        nc.tensor.matmul(bank[:], wv_sb[:, weight_cols], mentions_half[h][:])
                     staged = held.tile([P, HALF], F32, name=f"{part}_staged{b}{h}")
                     rows = out[row0 + b * P : row0 + (b + 1) * P, cols]
                     if h == 0:

@@ -8,6 +8,8 @@ N = 512
 M = 256
 BLOCKS = M // P
 HALF = N // 2
+QUARTER = N // 4
+BANKS = 8
 SCALE = 1.0 / math.sqrt(32.0)
 
 FLOPS = 2 * P * N * (2 * M)
@@ -23,13 +25,12 @@ def tile_glremodule_kernel(tc, sentences, wk, mentions, wv, offs, out):
     nc = tc.nc
     with (
         tc.tile_pool(name="held", bufs=1) as held,
-        tc.psum_pool(name="banks", bufs=1) as banks,
+        tc.psum_pool(name="banks", bufs=BANKS) as banks,
     ):
-        mentions_half = [held.tile([P, HALF], BF16, name=f"mentions_half{h}") for h in range(2)]
-        nc.sync.dma_start(mentions_half[0][:], mentions[:, 0:HALF])
+        mentions_sb = held.tile([P, N], BF16, name="mentions_sb")
+        nc.sync.dma_start(mentions_sb[:], mentions)
         wv_sb = held.tile([P, M], BF16, name="wv_sb")
         nc.scalar.dma_start(wv_sb[:], wv)
-        nc.scalar.dma_start(mentions_half[1][:], mentions[:, HALF:N])
         offsets = held.tile([P, N // 16], U16, name="offsets")
         nc.sync.dma_start(offsets[:], offs)
         wk_sb = held.tile([P, M], BF16, name="wk_sb")
@@ -37,22 +38,28 @@ def tile_glremodule_kernel(tc, sentences, wk, mentions, wv, offs, out):
         window = held.tile([P, S], BF16, name="window")
         nc.sync.dma_start(window[:], sentences)
 
-        for part, row0, scale in (("values", M, 1.0), ("keys", 0, SCALE)):
+        pieces = []
+        for part in ("values", "keys"):
             for b in range(BLOCKS):
-                weight_cols = slice(b * P, (b + 1) * P)
-                for h in range(2):
-                    cols = slice(h * HALF, (h + 1) * HALF)
-                    bank = banks.tile([P, HALF], F32, name=f"{part}_bank{b}{h}")
-                    if part == "keys":
-                        piece = offsets[:, h * (HALF // 16) : (h + 1) * (HALF // 16)]
-                        nc.tensor.matmul(bank[:], wk_sb[:, weight_cols], window[:].indirect(piece))
-                    else:
-                        nc.tensor.matmul(bank[:], wv_sb[:, weight_cols], mentions_half[h][:])
-                    staged = held.tile([P, HALF], F32, name=f"{part}_staged{b}{h}")
-                    rows = out[row0 + b * P : row0 + (b + 1) * P, cols]
-                    if h == 0:
-                        nc.vector.tensor_scalar_mul(staged[:], bank[:], scale)
-                        nc.sync.dma_start(rows, staged[:])
-                    else:
-                        nc.scalar.activation(staged[:], bank[:], COPY, scale=scale)
-                        nc.scalar.dma_start(rows, staged[:])
+                pieces.extend([(part, b, 0, HALF), (part, b, HALF, HALF)])
+        pieces.pop()
+        pieces.extend([("keys", BLOCKS - 1, HALF, QUARTER), ("keys", BLOCKS - 1, HALF + QUARTER, QUARTER)])
+
+        for i, (part, b, col0, width) in enumerate(pieces):
+            weight_cols = slice(b * P, (b + 1) * P)
+            bank = banks.tile([P, width], F32, name=f"bank{i}", tag="bank")
+            if part == "keys":
+                entries = offsets[:, col0 // 16 : (col0 + width) // 16]
+                nc.tensor.matmul(bank[:], wk_sb[:, weight_cols], window[:].indirect(entries))
+                row0, scale = 0, SCALE
+            else:
+                nc.tensor.matmul(bank[:], wv_sb[:, weight_cols], mentions_sb[:, col0 : col0 + width])
+                row0, scale = M, 1.0
+            staged = held.tile([P, width], F32, name=f"staged{i}")
+            rows = out[row0 + b * P : row0 + (b + 1) * P, col0 : col0 + width]
+            if i % 2 == 0:
+                nc.vector.tensor_scalar_mul(staged[:], bank[:], scale)
+                nc.sync.dma_start(rows, staged[:])
+            else:
+                nc.scalar.activation(staged[:], bank[:], COPY, scale=scale)
+                nc.scalar.dma_start(rows, staged[:])

@@ -57,9 +57,9 @@ def tile_glremodule_kernel(tc, sentences, wk, mentions, wv, offs, out):
                 row0, scale = M, 1.0
             staged = held.tile([P, width], F32, name=f"staged{i}")
             rows = out[row0 + b * P : row0 + (b + 1) * P, col0 : col0 + width]
-            if i % 2 == 0:
-                nc.vector.tensor_scalar_mul(staged[:], bank[:], scale)
-                nc.sync.dma_start(rows, staged[:])
-            else:
+            if col0 + width == N:
                 nc.scalar.activation(staged[:], bank[:], COPY, scale=scale)
                 nc.scalar.dma_start(rows, staged[:])
+            else:
+                nc.vector.tensor_scalar_mul(staged[:], bank[:], scale)
+                nc.sync.dma_start(rows, staged[:])

@@ -38,12 +38,9 @@ def tile_glremodule_kernel(tc, sentences, wk, mentions, wv, offs, out):
         window = held.tile([P, S], BF16, name="window")
         nc.sync.dma_start(window[:], sentences)
 
-        pieces = []
-        for part in ("values", "keys"):
-            for b in range(BLOCKS):
-                pieces.extend([(part, b, 0, HALF), (part, b, HALF, HALF)])
-        pieces.pop()
-        pieces.extend([("keys", BLOCKS - 1, HALF, QUARTER), ("keys", BLOCKS - 1, HALF + QUARTER, QUARTER)])
+        pieces = [(part, b, col0, HALF) for part in ("values", "keys") for b in range(BLOCKS) for col0 in (0, HALF)]
+        pieces[0:1] = [("values", 0, 0, QUARTER), ("values", 0, QUARTER, QUARTER)]
+        pieces[-1:] = [("keys", BLOCKS - 1, HALF, QUARTER), ("keys", BLOCKS - 1, HALF + QUARTER, QUARTER)]
 
         for i, (part, b, col0, width) in enumerate(pieces):
             weight_cols = slice(b * P, (b + 1) * P)

@@ -27,14 +27,14 @@ def tile_glremodule_kernel(tc, sentences, wk, mentions, wv, offs, out):
         tc.tile_pool(name="held", bufs=1) as held,
         tc.psum_pool(name="banks", bufs=BANKS) as banks,
     ):
+        wv_sb = held.tile([P, M], BF16, name="wv_sb")
+        nc.sync.dma_start(wv_sb[:], wv)
         mentions_sb = held.tile([P, N], BF16, name="mentions_sb")
         nc.sync.dma_start(mentions_sb[:], mentions)
-        wv_sb = held.tile([P, M], BF16, name="wv_sb")
-        nc.scalar.dma_start(wv_sb[:], wv)
         offsets = held.tile([P, N // 16], U16, name="offsets")
         nc.sync.dma_start(offsets[:], offs)
         wk_sb = held.tile([P, M], BF16, name="wk_sb")
-        nc.scalar.dma_start(wk_sb[:], wk)
+        nc.sync.dma_start(wk_sb[:], wk)
         window = held.tile([P, S], BF16, name="window")
         nc.sync.dma_start(window[:], sentences)
 

@@ -30,7 +30,8 @@ def tile_glremodule_kernel(tc, sentences, wk, mentions, wv, offs, out):
         wv_sb = held.tile([P, M], BF16, name="wv_sb")
         nc.sync.dma_start(wv_sb[:], wv)
         mentions_sb = held.tile([P, N], BF16, name="mentions_sb")
-        nc.sync.dma_start(mentions_sb[:], mentions)
+        nc.sync.dma_start(mentions_sb[:, 0:QUARTER], mentions[:, 0:QUARTER])
+        nc.sync.dma_start(mentions_sb[:, QUARTER:N], mentions[:, QUARTER:N])
         offsets = held.tile([P, N // 16], U16, name="offsets")
         nc.sync.dma_start(offsets[:], offs)
         wk_sb = held.tile([P, M], BF16, name="wk_sb")

@@ -55,7 +55,7 @@ def tile_glremodule_kernel(tc, sentences, wk, mentions, wv, offs, out):
                 row0, scale = M, 1.0
             staged = held.tile([P, width], F32, name=f"staged{i}")
             rows = out[row0 + b * P : row0 + (b + 1) * P, col0 : col0 + width]
-            if col0 + width == N:
+            if i % 2 == 1 and i > 1:
                 nc.scalar.activation(staged[:], bank[:], COPY, scale=scale)
                 nc.scalar.dma_start(rows, staged[:])
             else:

@@ -30,8 +30,8 @@ def tile_glremodule_kernel(tc, sentences, wk, mentions, wv, offs, out):
         wv_sb = held.tile([P, M], BF16, name="wv_sb")
         nc.sync.dma_start(wv_sb[:], wv)
         mentions_sb = held.tile([P, N], BF16, name="mentions_sb")
-        nc.sync.dma_start(mentions_sb[:, 0:QUARTER], mentions[:, 0:QUARTER])
-        nc.sync.dma_start(mentions_sb[:, QUARTER:N], mentions[:, QUARTER:N])
+        nc.sync.dma_start(mentions_sb[:, 0:HALF], mentions[:, 0:HALF])
+        nc.sync.dma_start(mentions_sb[:, HALF:N], mentions[:, HALF:N])
         offsets = held.tile([P, N // 16], U16, name="offsets")
         nc.sync.dma_start(offsets[:], offs)
         wk_sb = held.tile([P, M], BF16, name="wk_sb")

import math

import concourse.mybir as mybir

P = 128
S = 1024
N = 512
M = 256
BLOCKS = M // P
HALF = N // 2
QUARTER = N // 4
BANKS = 8
SCALE = 1.0 / math.sqrt(32.0)

FLOPS = 2 * P * N * (2 * M)
BYTES = 2 * (P * N + P * M + P * N + P * M) + 2 * P * (N // 16) + 4 * (2 * M) * N

BF16 = mybir.dt.bfloat16
F32 = mybir.dt.float32
U16 = mybir.dt.uint16
COPY = mybir.ActivationFunctionType.Copy


def tile_glremodule_kernel(tc, sentences, wk, mentions, wv, offs, out):
    nc = tc.nc
    with (
        tc.tile_pool(name="held", bufs=1) as held,
        tc.psum_pool(name="banks", bufs=BANKS) as banks,
    ):
        wv_sb = held.tile([P, M], BF16, name="wv_sb")
        nc.sync.dma_start(wv_sb[:], wv)
        mentions_sb = held.tile([P, N], BF16, name="mentions_sb")
        nc.sync.dma_start(mentions_sb[:, 0:HALF], mentions[:, 0:HALF])
        nc.sync.dma_start(mentions_sb[:, HALF:N], mentions[:, HALF:N])
        offsets = held.tile([P, N // 16], U16, name="offsets")
        nc.sync.dma_start(offsets[:], offs)
        wk_sb = held.tile([P, M], BF16, name="wk_sb")
        nc.sync.dma_start(wk_sb[:], wk)
        window = held.tile([P, S], BF16, name="window")
        nc.sync.dma_start(window[:], sentences)

        pieces = [(part, b, col0, HALF) for part in ("values", "keys") for b in range(BLOCKS) for col0 in (0, HALF)]
        pieces[0:1] = [("values", 0, 0, QUARTER), ("values", 0, QUARTER, QUARTER)]
        pieces[-1:] = [("keys", BLOCKS - 1, HALF, QUARTER), ("keys", BLOCKS - 1, HALF + QUARTER, QUARTER)]

        for i, (part, b, col0, width) in enumerate(pieces):
            weight_cols = slice(b * P, (b + 1) * P)
            bank = banks.tile([P, width], F32, name=f"bank{i}", tag="bank")
            if part == "keys":
                entries = offsets[:, col0 // 16 : (col0 + width) // 16]
                nc.tensor.matmul(bank[:], wk_sb[:, weight_cols], window[:].indirect(entries))
                row0, scale = 0, SCALE
            else:
                nc.tensor.matmul(bank[:], wv_sb[:, weight_cols], mentions_sb[:, col0 : col0 + width])
                row0, scale = M, 1.0
            staged = held.tile([P, width], F32, name=f"staged{i}")
            rows = out[row0 + b * P : row0 + (b + 1) * P, col0 : col0 + width]
            if i % 2 == 1 and i > 1:
                nc.scalar.activation(staged[:], bank[:], COPY, scale=scale)
                nc.scalar.dma_start(rows, staged[:])
            else:
                nc.vector.tensor_scalar_mul(staged[:], bank[:], scale)
                nc.sync.dma_start(rows, staged[:])
